import numpy as np
import ml_dtypes


def mxq(x, axis, fmt="e4m3"):
    dtype, down = {"e4m3": (ml_dtypes.float8_e4m3fn, 7), "e5m2": (ml_dtypes.float8_e5m2, 14)}[fmt]
    v = np.moveaxis(np.asarray(x, np.float32).astype(ml_dtypes.bfloat16).astype(np.float64), axis, -1)
    blocks = v.reshape(v.shape[:-1] + (-1, 32))
    amax = np.abs(blocks).max(-1, keepdims=True)
    byte = np.maximum(np.where(amax > 0, np.frexp(amax)[1] - 1 + 127, 0) - down, 1)
    scale = np.exp2(byte - 127.0)
    codes = (blocks / scale).astype(np.float32).astype(dtype).astype(np.float64)
    return np.moveaxis((codes * scale).reshape(v.shape), -1, axis)


WIDE = False


def mx_kscale(k):
    if not WIDE:
        return np.ones(k)
    levels = np.array([10, -10, 5, -5, 0])
    if k % 512:
        return np.exp2(np.random.permutation(np.resize(levels, k // 32))).repeat(32)
    a = np.empty((k // 512, 16))
    for p in range(k // 512):
        a[p, :8] = np.random.permutation(np.resize(levels, 8))
        for g in range(8):
            far = levels[np.abs(levels - a[p, g]) >= 10]
            a[p, g + 8] = far[np.random.randint(len(far))]
    return np.exp2(a.ravel()).repeat(32)


BF16 = ml_dtypes.bfloat16


def bf(x):
    return np.asarray(x, np.float32).astype(BF16)


def f64(x):
    return np.asarray(x).astype(np.float64)


B, S, E, LAT, H = 4, 2048, 512, 512, 4
D = E // H
R = D // 2
HR = H * R


def rope_cos_sin(n):
    inv_freq = 1.0 / (10000.0 ** (np.arange(0, R, 2) / R))
    freqs = np.outer(np.arange(n), inv_freq)
    emb = np.concatenate([freqs, freqs], axis=-1)
    return np.cos(emb), np.sin(emb)


def rotate_half(v):
    v1, v2 = v[..., : R // 2], v[..., R // 2 :]
    return np.concatenate([-v2, v1], axis=-1)


def apply_rope(v, cos, sin):
    return v * cos[None, :, None, :] + rotate_half(v) * sin[None, :, None, :]


def draw0():
    s, t = mx_kscale(E), mx_kscale(LAT)
    return {
        "x": bf(np.random.standard_normal((B, S, E)) * s),
        "Wq_d": bf(np.random.standard_normal((LAT, E)) / np.sqrt(E) * t[:, None] / s[None, :]),
        "bq_d": bf(np.random.standard_normal(LAT) * 0.3 * t),
        "Wq_u": bf(np.random.standard_normal((HR, LAT)) / np.sqrt(LAT) / t[None, :]),
        "bq_u": bf(np.random.standard_normal(HR) * 0.3),
        "Wrq": bf(np.random.standard_normal((HR, LAT)) / np.sqrt(LAT) / t[None, :]),
        "brq": bf(np.random.standard_normal(HR) * 0.3),
    }


def core(x, Wq_d, bq_d, Wq_u, bq_u, Wrq, brq):
    q_d = (mxq(f64(x), 2, "e4m3") @ mxq(f64(Wq_d), 1, "e4m3").T) + f64(bq_d)
    qdq = mxq(q_d, 2, "e4m3")
    q1 = ((qdq @ mxq(f64(Wq_u), 1, "e4m3").T) + f64(bq_u)).reshape(B, S, H, R)
    qr = ((qdq @ mxq(f64(Wrq), 1, "e4m3").T) + f64(brq)).reshape(B, S, H, R)
    cos, sin = rope_cos_sin(S)
    qr = apply_rope(qr, cos, sin)
    return np.concatenate([q1, qr], axis=-1)


def e4m3fn_bytes(y):
    return np.clip(np.asarray(y, np.float64), -448.0, 448.0).astype(np.float32).astype(ml_dtypes.float8_e4m3fn).view(np.uint8)


def e4m3fn_values(b):
    return np.asarray(b, np.uint8).view(ml_dtypes.float8_e4m3fn).astype(np.float64)


def setup_inputs():
    d = draw0()
    x0 = np.asarray(d['x']).astype(np.float64)
    s = (np.max(np.abs(x0), axis=(0, 1), keepdims=True) / 448.0).astype(np.float32)
    out = {}
    for k, v in d.items():
        if k == 'x':
            out['x_bytes'] = e4m3fn_bytes(x0 / s.astype(np.float64))
            out['x_scale'] = s
        else:
            out[k] = v
    return out


def reference(x_bytes, x_scale, Wq_d, bq_d, Wq_u, bq_u, Wrq, brq):
    return core(e4m3fn_values(x_bytes) * x_scale.astype(np.float64), Wq_d, bq_d, Wq_u, bq_u, Wrq, brq)

@@ -1,0 +1,336 @@
+import math
+from contextlib import ExitStack
+
+import concourse.mybir as mybir
+from concourse.masks import make_identity
+
+F32 = mybir.dt.float32
+BF16 = mybir.dt.bfloat16
+I32 = mybir.dt.int32
+U32 = mybir.dt.uint32
+U8 = mybir.dt.uint8
+FP8 = mybir.dt.float8_e4m3fn
+FP8X4 = mybir.dt.float8_e4m3fn_x4
+ADD = mybir.AluOpType.add
+SUB = mybir.AluOpType.subtract
+MULT = mybir.AluOpType.mult
+ACT = mybir.ActivationFunctionType
+
+P = 128
+B, S, E, LAT, H = 4, 2048, 512, 512, 4
+GT = 512
+CH = S // GT
+FLOPS = 2 * B * S * E * LAT * 2
+
+ORDER = (
+    ("TT",0,0),
+    ("A",2,0),
+    ("TT",0,1),
+    ("A",2,1),
+    ("p",2,0),
+    ("O",4,0),
+    ("C",3,0),
+    ("C",3,4),
+    ("p",2,1),
+    ("A",2,2),
+    ("q",3,0),
+    ("A",2,3),
+    ("o",4,0),
+    ("p",2,2),
+    ("C",3,3),
+    ("O",4,1),
+    ("X",0,0),
+    ("p",2,3),
+    ("qx",1),
+    ("O",4,2),
+    ("T",3,4,0),
+    ("X",0,1),
+    ("C",3,2),
+    ("T",3,3,0),
+    ("I",2),
+    ("o",4,1),
+    ("T",3,2,0),
+    ("qq",2),
+    ("C",3,1),
+    ("xe",0,0),
+    ("O",4,3),
+    ("o",4,2),
+    ("xe",0,1),
+    ("q",3,1),
+    ("o",4,3),
+)
+
+
+def tile_multiheadlatentattention_pa_t_kernel(
+    tc, x_bytes, x_scale, Wq_d, bq_d, Wq_u, bq_u, Wrq, brq, out
+):
+    nc = tc.nc
+    with ExitStack() as ctx:
+        keep = ctx.enter_context(tc.tile_pool(name="keep", bufs=1))
+        xin = ctx.enter_context(tc.tile_pool(name="xin", bufs=16))
+        work = ctx.enter_context(tc.tile_pool(name="work", bufs=2))
+        psum = ctx.enter_context(tc.psum_pool(name="psum", bufs=2))
+        ctx.enter_context(tc.manual_schedule())
+
+        xb_view = x_bytes.rearrange("b (c p a) k -> b c p (a k)", c=CH, p=P, a=4)
+        out_view = out.rearrange("b (c p a) h d -> b c p (a h d)", c=CH, p=P, a=4)
+        groups = [(c, b) for c in range(CH) for b in range(B)]
+        n = len(groups)
+
+        xb = {}
+
+        def load_x(g):
+            c, b = groups[g]
+            t = xin.tile([P, 4 * E], U8, name="xb", align_bytes=64)
+            nc.sync.dma_start(out=t[:], in_=xb_view[b, c])
+            xb[g] = t
+
+        sc4 = keep.tile([P, 4], F32)
+        nc.scalar.dma_start(out=sc4[:], in_=x_scale.rearrange("o u (c p) -> p (o u c)", p=P))
+        bd_raw = keep.tile([P, 4], BF16)
+        nc.scalar.dma_start(out=bd_raw[:], in_=bq_d.rearrange("(p j) -> p j", j=4))
+        wd = keep.tile([P, 4 * E], BF16, align_bytes=64)
+        load_x(0)
+        nc.sync.dma_start(out=wd[:], in_=Wq_d.rearrange("(m t) k -> m (t k)", t=4))
+        load_x(1)
+        b2_rows = keep.tile([P, P], BF16)
+        nc.vector.memset(b2_rows[:], 0.0)
+        w2 = keep.tile([P, 4, LAT], BF16, align_bytes=64)
+        for v, (w, bv) in enumerate(((Wq_u, bq_u), (Wrq, brq))):
+            nc.scalar.dma_start(
+                out=b2_rows[2 * v : 2 * v + 2, :].rearrange("s (h i) -> s h i", h=H),
+                in_=bv.rearrange("(h s i) -> s h i", h=H, s=2),
+            )
+            for h in range(H):
+                nc.sync.dma_start(
+                    out=w2[32 * h : 32 * (h + 1), 2 * v : 2 * v + 2, :],
+                    in_=w.rearrange("(h s i) k -> h i s k", h=H, s=2)[h],
+                )
+        for g in range(2, n):
+            load_x(g)
+
+        ident = keep.tile([P, P], F32)
+        make_identity(nc, ident[:])
+        part = keep.tile([P, 1], F32)
+        nc.gpsimd.iota(part[:], pattern=[[0, 1]], base=0, channel_multiplier=1, allow_small_or_imprecise_dtypes=True)
+        base = keep.tile([P, 1], F32)
+        nc.gpsimd.memset(base[:], 10000.0)
+        pos = keep.tile([P, 4, P], F32)
+        nc.gpsimd.iota(pos[:], pattern=[[1, 4], [4, P]], base=0, channel_multiplier=0, allow_small_or_imprecise_dtypes=True)
+        GE = mybir.AluOpType.is_ge
+        jt = [keep.tile([P, 1], F32, name=f"jt{i}") for i in range(3)]
+        for i in range(3):
+            nc.vector.tensor_scalar(out=jt[i][:], in0=part[:], scalar1=32.0 * (i + 1), scalar2=1.0, op0=GE, op1=MULT)
+        nc.vector.tensor_tensor(out=jt[0][:], in0=jt[0][:], in1=jt[1][:], op=ADD)
+        nc.vector.tensor_tensor(out=jt[0][:], in0=jt[0][:], in1=jt[2][:], op=ADD)
+        jm = keep.tile([P, 1], F32)
+        nc.vector.scalar_tensor_tensor(out=jm[:], in0=jt[0][:], scalar=-32.0, in1=part[:], op0=MULT, op1=ADD)
+        nc.vector.tensor_scalar(out=jm[:], in0=jm[:], scalar1=-1.0 / 32, scalar2=None, op0=MULT)
+        wpow = keep.tile([P, 1], F32)
+        nc.gpsimd.tensor_tensor(out=wpow[:], in0=base[:], in1=jm[:], op=mybir.AluOpType.pow)
+        wcol = keep.tile([P, 1], F32)
+        nc.gpsimd.tensor_scalar(out=wcol[:], in0=wpow[:], scalar1=1 / (2 * math.pi), scalar2=0.0, op0=MULT, op1=ADD)
+        tb = {}
+
+        def table1(c):
+            t = work.tile([P, GT], F32, name="tb_t")
+            nc.gpsimd.tensor_scalar(
+                out=t[:], in0=pos[:].rearrange("p a n -> p (a n)"), scalar1=float(GT * c), scalar2=wcol[:], op0=ADD, op1=MULT
+            )
+            ni = work.tile([P, GT], I32, name="tb_i")
+            nc.vector.tensor_copy(out=ni[:], in_=t[:])
+            tb[c] = (t, ni)
+
+        def table2(c):
+            t, ni = tb[c]
+            nf = work.tile([P, GT], F32, name="tb_f")
+            nc.vector.tensor_copy(out=nf[:], in_=ni[:])
+            u = work.tile([P, GT], F32, name="tb_u")
+            nc.gpsimd.tensor_tensor(out=u[:], in0=t[:], in1=nf[:], op=SUB)
+            tb[c] = u
+
+        def table3(c):
+            u = tb[c]
+            sn = work.tile([P, GT], F32, name="tb_s")
+            nc.scalar.activation(out=sn[:], in_=u[:], func=ACT.Sin, scale=2 * math.pi)
+            hs = work.tile([P, GT], F32, name="tb_h")
+            nc.scalar.activation(out=hs[:], in_=u[:], func=ACT.Sin, scale=math.pi)
+            sq = work.tile([P, GT], F32, name="tb_q")
+            nc.gpsimd.tensor_tensor(out=sq[:], in0=hs[:], in1=hs[:], op=MULT)
+            cs = work.tile([P, GT], F32, name="tb_cos")
+            nc.gpsimd.tensor_scalar(out=cs[:], in0=sq[:], scalar1=-2.0, scalar2=1.0, op0=MULT, op1=ADD)
+            ncs = work.tile([P, GT], F32, name="tb_nc")
+            nc.gpsimd.tensor_scalar(out=ncs[:], in0=sq[:], scalar1=2.0, scalar2=-1.0, op0=MULT, op1=ADD)
+            t2 = work.tile([P, GT], F32, name="tb_smc")
+            nc.gpsimd.tensor_tensor(out=t2[:], in0=sn[:], in1=ncs[:], op=ADD)
+            t3 = work.tile([P, GT], F32, name="tb_mcs")
+            nc.gpsimd.tensor_tensor(out=t3[:], in0=ncs[:], in1=sn[:], op=SUB)
+            tb[c] = {4: cs, 2: t2, 3: t3}
+
+        def turn_half(words2, step8, xt):
+            for a in range(2):
+                for u in range(2):
+                    blk = words2[:, 256 * a : 256 * (a + 1)]
+                    if step8:
+                        src = blk.rearrange("p (q u i) -> p u q i", u=2, i=8)[:, u]
+                    else:
+                        src = blk[:, u::2]
+                    nc.tensor.transpose(xt[:, a, u, :], src, ident[:])
+
+        def turn_out(grouped, i, xt):
+            nc.scalar.copy(
+                out=grouped[:].bitcast(F32)[:, 512 * i : 512 * (i + 1)].rearrange("p (a n u) -> p a n u", a=2, u=2),
+                in_=xt[:].rearrange("p a u n -> p a n u"),
+            )
+
+        def quant(grouped, pool, name, bufs):
+            codes = pool.tile([P, GT], U32, name=name + "_c", align_bytes=64, bufs=bufs)
+            scales = pool.tile([P, GT], U8, name=name + "_s", align_bytes=64, bufs=bufs)
+            nc.vector.quantize_mx(out=codes[:].bitcast(FP8X4), scales=scales[:], in_=grouped[:])
+            return codes, scales
+
+        def mx(ps, w, m, r, start=True, stop=True):
+            nc.tensor.matmul_mx(
+                out=ps[:],
+                lhsT=w[0][:, m * P : (m + 1) * P].bitcast(FP8X4),
+                lhsT_scale=w[1][:, m * P : (m + 1) * P],
+                rhs=r[0][:].bitcast(FP8X4),
+                rhs_scale=r[1][:],
+                start=start,
+                stop=stop,
+            )
+
+        def weights(src, step8, name):
+            wg = work.tile([P, 4 * E], BF16, name="xg", align_bytes=64, bufs=3)
+            for i in range(2):
+                xt = psum.tile([P, 2, 2, P], F32, name="xt")
+                turn_half(src.bitcast(F32)[:, 512 * i : 512 * (i + 1)], step8, xt)
+                turn_out(wg, i, xt)
+            return quant(wg, keep, name, 1)
+
+        scp = psum.tile([P, 2, 2, P], F32, name="xt")
+        for c in range(4):
+            nc.tensor.transpose(scp[:, c // 2, c % 2, :], sc4[:, c : c + 1].to_broadcast([P, P]), ident[:])
+        sc = keep.tile([P, 2 * E], F32, align_bytes=64)
+        for r in range(2):
+            nc.scalar.copy(out=sc[:, r * E : (r + 1) * E], in_=scp[:].rearrange("p a u n -> p (a u n)"))
+
+        bd = keep.tile([P, 4], F32)
+        nc.vector.tensor_copy(out=bd[:], in_=bd_raw[:])
+        b2 = keep.tile([P, 5], F32)
+        wts = {}
+
+        def prep2():
+            ident_b = keep.tile([P, P], BF16)
+            nc.vector.tensor_copy(out=ident_b[:], in_=ident[:])
+            bps = psum.tile([P, P], BF16, name="ot")
+            nc.tensor.transpose(bps[:], b2_rows[:], ident_b[:])
+            nc.vector.tensor_copy(out=b2[:, 0:4], in_=bps[:, 0:4])
+            wts["w2"] = weights(w2[:].rearrange("p m k -> p (m k)"), False, "w2")
+            nc.vector.tensor_tensor(out=b2[:, 4:5], in0=b2[:, 2:3], in1=b2[:, 3:4], op=ADD)
+
+        xs, xt, xg, xq, s1, qp, qi, qq, s2, q1, km, ot, o_sb = ({} for i in range(13))
+
+        def f_TT(g, i):
+            xs[g, i] = work.tile([P, 2 * E], BF16, name="xs", align_bytes=64, bufs=4)
+            nc.vector.tensor_tensor(
+                out=xs[g, i][:], in0=xb[g][:, 1024 * i : 1024 * (i + 1)].bitcast(FP8), in1=sc[:], op=MULT
+            )
+
+        def f_X(g, i):
+            xt[g, i] = psum.tile([P, 2, 2, P], F32, name="xt")
+            turn_half(xs[g, i][:].bitcast(F32), False, xt[g, i])
+
+        def f_xe(g, i):
+            if i == 0:
+                xg[g] = work.tile([P, 4 * E], BF16, name="xg", align_bytes=64, bufs=3)
+            turn_out(xg[g], i, xt[g, i])
+
+        def f_qx(g):
+            xq[g] = quant(xg[g], work, "xq", 3)
+
+        def f_A(g, j):
+            s1[g, j] = psum.tile([P, GT], F32, name="s1")
+            mx(s1[g, j], wts["wd"], j, xq[g])
+
+        def f_p(g, j):
+            if j == 0:
+                qp[g] = work.tile([P, 4, GT], BF16, name="qp", align_bytes=64)
+            nc.scalar.activation(out=qp[g][:, j, :], in_=s1[g, j][:], func=ACT.Identity, bias=bd[:, j : j + 1])
+
+        def f_I(g):
+            qi[g] = work.tile([P, 4 * GT], BF16, name="qi", align_bytes=64)
+            nc.vector.tensor_copy(
+                out=qi[g][:].rearrange("p (c i t) -> p c t i", i=4, t=4), in_=qp[g][:].rearrange("p t (c i) -> p c t i", i=4)
+            )
+
+        def f_qq(g):
+            qq[g] = quant(qi[g], work, "qq", 2)
+
+        def f_C(g, k):
+            s2[g, k] = psum.tile([P, GT], F32, name="s2")
+            if k < 4:
+                mx(s2[g, k], wts["w2"], k, qq[g])
+            else:
+                mx(s2[g, k], wts["w2"], 2, qq[g], stop=False)
+                mx(s2[g, k], wts["w2"], 3, qq[g], start=False)
+
+        def f_q(g, k):
+            q1[g, k] = work.tile([P, GT], F32, name="q1", bufs=4)
+            nc.scalar.activation(out=q1[g, k][:], in_=s2[g, k][:], func=ACT.Identity, bias=b2[:, k : k + 1])
+
+        def f_T(g, k, unused):
+            km[g, k] = work.tile([P, GT], F32, name="km", bufs=8)
+            nc.vector.scalar_tensor_tensor(
+                out=km[g, k][:], in0=s2[g, k][:], scalar=b2[:, k : k + 1], in1=tb[groups[g][0]][k][:], op0=ADD, op1=MULT
+            )
+
+        def f_O(g, a):
+            cols = slice(a * P, (a + 1) * P)
+            t = psum.tile([P, 4, P], F32, name="ot")
+            for k in range(2):
+                nc.tensor.transpose(t[:, k, :], q1[g, k][:, cols], ident[:])
+            for k in (2, 3):
+                nc.tensor.matmul(t[:, k, :], lhsT=km[g, 4][:, cols], rhs=ident[:], start=True, stop=False, is_transpose=True)
+                nc.tensor.matmul(t[:, k, :], lhsT=km[g, 5 - k][:, cols], rhs=ident[:], start=False, stop=True, is_transpose=True)
+            ot[g, a] = t
+
+        done = {}
+
+        def f_o(g, a):
+            if g not in o_sb:
+                o_sb[g] = work.tile([P, 4, E], F32, name="o_sb", bufs=3)
+                done[g] = 0
+            src = ot[g, a][:].rearrange("p t (h i) -> p h t i", h=H)
+            dst = o_sb[g][:, a, :].rearrange("p (h t i) -> p h t i", h=H, t=4)
+            if a == 3 and g % 4 < 2:
+                nc.vector.tensor_copy(out=dst, in_=src)
+            else:
+                nc.scalar.copy(out=dst, in_=src)
+            done[g] += 1
+            if done[g] == 4:
+                c, b = groups[g]
+                nc.sync.dma_start(out=out_view[b, c], in_=o_sb[g][:].rearrange("p a f -> p (a f)"))
+
+        steps = {"TT": f_TT, "X": f_X, "xe": f_xe, "qx": f_qx, "A": f_A, "p": f_p, "I": f_I, "qq": f_qq, "C": f_C, "q": f_q, "T": f_T, "O": f_O, "o": f_o}
+
+        wts["wd"] = weights(wd[:], False, "wd")
+        for s in range(-3, n + 7):
+            c = s // 4
+            if 0 <= s < n:
+                if s == 0:
+                    table1(0)
+                    table2(0)
+                elif s % 4 == 0:
+                    table1(c)
+                elif s % 4 == 1:
+                    if s == 1:
+                        prep2()
+                    else:
+                        table2(c)
+                elif s % 4 == 2:
+                    table3(c)
+            for name, lag, *args in ORDER:
+                g = s - lag
+                if 0 <= g < n:
+                    steps[name](g, *args)

@@ -23,41 +23,41 @@ CH = S // GT
 FLOPS = 2 * B * S * E * LAT * 2
 
 ORDER = (
-    ("TT",0,0),
     ("A",2,0),
-    ("TT",0,1),
     ("A",2,1),
     ("p",2,0),
     ("O",4,0),
     ("C",3,0),
     ("C",3,4),
+    ("qx",1),
     ("p",2,1),
-    ("A",2,2),
-    ("q",3,0),
     ("A",2,3),
-    ("o",4,0),
-    ("p",2,2),
+    ("A",2,2),
+    ("T",3,4,0),
+    ("q",3,0),
     ("C",3,3),
-    ("O",4,1),
+    ("T",3,3,0),
     ("X",0,0),
     ("p",2,3),
-    ("qx",1),
-    ("O",4,2),
-    ("T",3,4,0),
-    ("X",0,1),
-    ("C",3,2),
-    ("T",3,3,0),
-    ("I",2),
-    ("o",4,1),
-    ("T",3,2,0),
-    ("qq",2),
+    ("p",2,2),
+    ("o",4,0),
+    ("O",4,1),
     ("C",3,1),
+    ("I",2),
+    ("C",3,2),
+    ("T",3,2,0),
+    ("O",4,2),
+    ("o",4,1),
     ("xe",0,0),
-    ("O",4,3),
-    ("o",4,2),
-    ("xe",0,1),
     ("q",3,1),
+    ("o",4,2),
+    ("X",0,1),
+    ("O",4,3),
+    ("qq",2),
+    ("xe",0,1),
+    ("TT",-1,0),
     ("o",4,3),
+    ("TT",-1,1),
 )
 
 
@@ -106,7 +106,7 @@ def tile_multiheadlatentattention_pa_t_kernel(
                     out=w2[32 * h : 32 * (h + 1), 2 * v : 2 * v + 2, :],
                     in_=w.rearrange("(h s i) k -> h i s k", h=H, s=2)[h],
                 )
-        for g in range(2, n):
+        for g in range(2, 6):
             load_x(g)
 
         ident = keep.tile([P, P], F32)
@@ -120,52 +120,49 @@ def tile_multiheadlatentattention_pa_t_kernel(
         GE = mybir.AluOpType.is_ge
         jt = [keep.tile([P, 1], F32, name=f"jt{i}") for i in range(3)]
         for i in range(3):
-            nc.vector.tensor_scalar(out=jt[i][:], in0=part[:], scalar1=32.0 * (i + 1), scalar2=1.0, op0=GE, op1=MULT)
+            nc.vector.tensor_scalar(out=jt[i][:], in0=part[:], scalar1=32.0 * (i + 1), scalar2=float(GT), op0=GE, op1=MULT)
+        quarter = keep.tile([P, 1], F32)
         nc.vector.tensor_tensor(out=jt[0][:], in0=jt[0][:], in1=jt[1][:], op=ADD)
-        nc.vector.tensor_tensor(out=jt[0][:], in0=jt[0][:], in1=jt[2][:], op=ADD)
+        nc.vector.tensor_tensor(out=quarter[:], in0=jt[0][:], in1=jt[2][:], op=ADD)
         jm = keep.tile([P, 1], F32)
-        nc.vector.scalar_tensor_tensor(out=jm[:], in0=jt[0][:], scalar=-32.0, in1=part[:], op0=MULT, op1=ADD)
-        nc.vector.tensor_scalar(out=jm[:], in0=jm[:], scalar1=-1.0 / 32, scalar2=None, op0=MULT)
+        nc.vector.scalar_tensor_tensor(out=jm[:], in0=quarter[:], scalar=-32.0 / GT, in1=part[:], op0=MULT, op1=ADD)
+        jn = keep.tile([P, 1], F32)
+        nc.vector.tensor_scalar(out=jn[:], in0=jm[:], scalar1=-1.0 / 32, scalar2=None, op0=MULT)
         wpow = keep.tile([P, 1], F32)
-        nc.gpsimd.tensor_tensor(out=wpow[:], in0=base[:], in1=jm[:], op=mybir.AluOpType.pow)
+        nc.gpsimd.tensor_tensor(out=wpow[:], in0=base[:], in1=jn[:], op=mybir.AluOpType.pow)
         wcol = keep.tile([P, 1], F32)
         nc.gpsimd.tensor_scalar(out=wcol[:], in0=wpow[:], scalar1=1 / (2 * math.pi), scalar2=0.0, op0=MULT, op1=ADD)
-        tb = {}
+        scratch = out[B - 1, S - GT : S].rearrange("(k r) h d -> k r (h d)", k=4)
+        tt = {k: keep.tile([P, GT], F32, name=f"tt_{k}") for k in ("t", "f", "u", "sn", "hs", "hh", "c", "smc", "mcs")}
+        tt_i = keep.tile([P, GT], I32)
+        tab = {k: keep.tile([P, CH, GT], F32, name=f"tab{k}") for k in (4, 2, 3)}
 
-        def table1(c):
-            t = work.tile([P, GT], F32, name="tb_t")
-            nc.gpsimd.tensor_scalar(
-                out=t[:], in0=pos[:].rearrange("p a n -> p (a n)"), scalar1=float(GT * c), scalar2=wcol[:], op0=ADD, op1=MULT
+        def angles():
+            nc.vector.tensor_scalar(
+                out=tt["t"][:], in0=pos[:].rearrange("p a n -> p (a n)"), scalar1=quarter[:], scalar2=wcol[:], op0=ADD, op1=MULT
             )
-            ni = work.tile([P, GT], I32, name="tb_i")
-            nc.vector.tensor_copy(out=ni[:], in_=t[:])
-            tb[c] = (t, ni)
+            nc.vector.tensor_copy(out=tt_i[:], in_=tt["t"][:])
+            nc.vector.tensor_copy(out=tt["f"][:], in_=tt_i[:])
+            nc.vector.tensor_tensor(out=tt["u"][:], in0=tt["t"][:], in1=tt["f"][:], op=SUB)
+            nc.scalar.activation(out=tt["hs"][:], in_=tt["u"][:], func=ACT.Sin, scale=math.pi)
+            nc.scalar.activation(out=tt["sn"][:], in_=tt["u"][:], func=ACT.Sin, scale=2 * math.pi)
 
-        def table2(c):
-            t, ni = tb[c]
-            nf = work.tile([P, GT], F32, name="tb_f")
-            nc.vector.tensor_copy(out=nf[:], in_=ni[:])
-            u = work.tile([P, GT], F32, name="tb_u")
-            nc.gpsimd.tensor_tensor(out=u[:], in0=t[:], in1=nf[:], op=SUB)
-            tb[c] = u
-
-        def table3(c):
-            u = tb[c]
-            sn = work.tile([P, GT], F32, name="tb_s")
-            nc.scalar.activation(out=sn[:], in_=u[:], func=ACT.Sin, scale=2 * math.pi)
-            hs = work.tile([P, GT], F32, name="tb_h")
-            nc.scalar.activation(out=hs[:], in_=u[:], func=ACT.Sin, scale=math.pi)
-            sq = work.tile([P, GT], F32, name="tb_q")
-            nc.gpsimd.tensor_tensor(out=sq[:], in0=hs[:], in1=hs[:], op=MULT)
-            cs = work.tile([P, GT], F32, name="tb_cos")
-            nc.gpsimd.tensor_scalar(out=cs[:], in0=sq[:], scalar1=-2.0, scalar2=1.0, op0=MULT, op1=ADD)
-            ncs = work.tile([P, GT], F32, name="tb_nc")
-            nc.gpsimd.tensor_scalar(out=ncs[:], in0=sq[:], scalar1=2.0, scalar2=-1.0, op0=MULT, op1=ADD)
-            t2 = work.tile([P, GT], F32, name="tb_smc")
-            nc.gpsimd.tensor_tensor(out=t2[:], in0=sn[:], in1=ncs[:], op=ADD)
-            t3 = work.tile([P, GT], F32, name="tb_mcs")
-            nc.gpsimd.tensor_tensor(out=t3[:], in0=ncs[:], in1=sn[:], op=SUB)
-            tb[c] = {4: cs, 2: t2, 3: t3}
+        def tables():
+            STT = nc.vector.scalar_tensor_tensor
+            STT(out=tt["hh"][:], in0=tt["hs"][:], scalar=-2.0, in1=tt["hs"][:], op0=MULT, op1=MULT)
+            nc.vector.tensor_scalar(out=tt["c"][:], in0=tt["hh"][:], scalar1=1.0, scalar2=None, op0=ADD)
+            STT(out=tt["smc"][:], in0=tt["c"][:], scalar=-1.0, in1=tt["sn"][:], op0=MULT, op1=ADD)
+            STT(out=tt["mcs"][:], in0=tt["c"][:], scalar=-1.0, in1=tt["sn"][:], op0=MULT, op1=SUB)
+            src = {4: "c", 2: "smc", 3: "mcs"}
+            for i, k in enumerate((4, 2, 3)):
+                nc.sync.dma_start(out=scratch[i], in_=tt[src[k]][:])
+            for lo, hi in ((0, 1), (1, CH)):
+                for i, k in enumerate((4, 2, 3)):
+                    for h in range(H):
+                        nc.sync.dma_start(
+                            out=tab[k][32 * h : 32 * (h + 1), lo:hi, :],
+                            in_=scratch[i][32 * lo : 32 * hi, :].rearrange("(c j) n -> j c n", j=32),
+                        )
 
         def turn_half(words2, step8, xt):
             for a in range(2):
@@ -282,7 +279,7 @@ def tile_multiheadlatentattention_pa_t_kernel(
         def f_T(g, k, unused):
             km[g, k] = work.tile([P, GT], F32, name="km", bufs=8)
             nc.vector.scalar_tensor_tensor(
-                out=km[g, k][:], in0=s2[g, k][:], scalar=b2[:, k : k + 1], in1=tb[groups[g][0]][k][:], op0=ADD, op1=MULT
+                out=km[g, k][:], in0=s2[g, k][:], scalar=b2[:, k : k + 1], in1=tab[k][:, groups[g][0], :], op0=ADD, op1=MULT
             )
 
         def f_O(g, a):
@@ -314,22 +311,15 @@ def tile_multiheadlatentattention_pa_t_kernel(
 
         steps = {"TT": f_TT, "X": f_X, "xe": f_xe, "qx": f_qx, "A": f_A, "p": f_p, "I": f_I, "qq": f_qq, "C": f_C, "q": f_q, "T": f_T, "O": f_O, "o": f_o}
 
+        angles()
         wts["wd"] = weights(wd[:], False, "wd")
         for s in range(-3, n + 7):
-            c = s // 4
-            if 0 <= s < n:
-                if s == 0:
-                    table1(0)
-                    table2(0)
-                elif s % 4 == 0:
-                    table1(c)
-                elif s % 4 == 1:
-                    if s == 1:
-                        prep2()
-                    else:
-                        table2(c)
-                elif s % 4 == 2:
-                    table3(c)
+            if s == 0:
+                tables()
+                for g in range(6, n):
+                    load_x(g)
+            if s == 1:
+                prep2()
             for name, lag, *args in ORDER:
                 g = s - lag
                 if 0 <= g < n:

@@ -2,7 +2,6 @@ import math
 from contextlib import ExitStack
 
 import concourse.mybir as mybir
-from concourse.masks import make_identity
 
 F32 = mybir.dt.float32
 BF16 = mybir.dt.bfloat16
@@ -11,54 +10,61 @@ U32 = mybir.dt.uint32
 U8 = mybir.dt.uint8
 FP8 = mybir.dt.float8_e4m3fn
 FP8X4 = mybir.dt.float8_e4m3fn_x4
-ADD = mybir.AluOpType.add
-SUB = mybir.AluOpType.subtract
-MULT = mybir.AluOpType.mult
+ALU = mybir.AluOpType
 ACT = mybir.ActivationFunctionType
 
 P = 128
 B, S, E, LAT, H = 4, 2048, 512, 512, 4
-GT = 512
-CH = S // GT
-FLOPS = 2 * B * S * E * LAT * 2
+FREQS = 32
+GROUP = 512
+TILES = GROUP // P
+QUARTERS = S // GROUP
+GROUPS = [(quarter, b) for quarter in range(QUARTERS) for b in range(B)]
+SUM = 4
+FLOPS = 2 * B * S * LAT * (E + H * 2 * 2 * FREQS)
+
+EARLY_LOADS = 6
+
+DIRECT = (14, 15)
 
 ORDER = (
-    ("A",2,0),
-    ("A",2,1),
-    ("p",2,0),
-    ("O",4,0),
-    ("C",3,0),
-    ("C",3,4),
-    ("qx",1),
-    ("p",2,1),
-    ("A",2,3),
-    ("A",2,2),
-    ("T",3,4,0),
-    ("q",3,0),
-    ("C",3,3),
-    ("T",3,3,0),
-    ("X",0,0),
-    ("p",2,3),
-    ("p",2,2),
-    ("o",4,0),
-    ("O",4,1),
-    ("C",3,1),
-    ("I",2),
-    ("C",3,2),
-    ("T",3,2,0),
-    ("O",4,2),
-    ("o",4,1),
-    ("xe",0,0),
-    ("q",3,1),
-    ("o",4,2),
-    ("X",0,1),
-    ("O",4,3),
-    ("qq",2),
-    ("xe",0,1),
-    ("TT",-1,0),
-    ("o",4,3),
-    ("TT",-1,1),
+    ("down", 2, 1),
+    ("latent", 2, 1),
+    ("down", 2, 0),
+    ("latent", 2, 0),
+    ("turn_back", 4, 0),
+    ("up", 3, 0),
+    ("quantise_x", 1),
+    ("bias_q1", 3, 0),
+    ("store", 4, 0),
+    ("up", 3, 4),
+    ("down", 2, 2),
+    ("turn_back", 4, 1),
+    ("rotate", 3, 4),
+    ("down", 2, 3),
+    ("up", 3, 3),
+    ("latent", 2, 2),
+    ("rotate", 3, 3),
+    ("latent", 2, 3),
+    ("turn_x", 0, 0),
+    ("interleave", 2),
+    ("turn_back", 4, 2),
+    ("store", 4, 1),
+    ("turn_x", 0, 1),
+    ("empty_x", 0, 0),
+    ("up", 3, 1),
+    ("store", 4, 2),
+    ("up", 3, 2),
+    ("rotate", 3, 2),
+    ("bias_q1", 3, 1),
+    ("turn_back", 4, 3),
+    ("empty_x", 0, 1),
+    ("quantise_q", 2),
+    ("store", 4, 3),
+    ("scale_x", -1, 0),
+    ("scale_x", -1, 1),
 )
+LAGS = [item[1] for item in ORDER]
 
 
 def tile_multiheadlatentattention_pa_t_kernel(
@@ -67,260 +73,355 @@ def tile_multiheadlatentattention_pa_t_kernel(
     nc = tc.nc
     with ExitStack() as ctx:
         keep = ctx.enter_context(tc.tile_pool(name="keep", bufs=1))
-        xin = ctx.enter_context(tc.tile_pool(name="xin", bufs=16))
+        bytes_in = ctx.enter_context(tc.tile_pool(name="bytes_in", bufs=len(GROUPS)))
         work = ctx.enter_context(tc.tile_pool(name="work", bufs=2))
         psum = ctx.enter_context(tc.psum_pool(name="psum", bufs=2))
         ctx.enter_context(tc.manual_schedule())
 
-        xb_view = x_bytes.rearrange("b (c p a) k -> b c p (a k)", c=CH, p=P, a=4)
-        out_view = out.rearrange("b (c p a) h d -> b c p (a h d)", c=CH, p=P, a=4)
-        groups = [(c, b) for c in range(CH) for b in range(B)]
-        n = len(groups)
+        one = keep.tile([P, 1], F32)
+        nc.vector.memset(one[:], 1.0)
+        base = keep.tile([P, 1], F32)
+        nc.vector.memset(base[:], 10000.0)
 
-        xb = {}
+        x_view = x_bytes.rearrange("b (q p a) k -> b q p (a k)", q=QUARTERS, a=TILES)
+        out_view = out.rearrange("b (q p a) h d -> b q p (a h d)", q=QUARTERS, a=TILES)
+        x_in = {}
 
         def load_x(g):
-            c, b = groups[g]
-            t = xin.tile([P, 4 * E], U8, name="xb", align_bytes=64)
-            nc.sync.dma_start(out=t[:], in_=xb_view[b, c])
-            xb[g] = t
+            quarter, b = GROUPS[g]
+            tile = bytes_in.tile([P, TILES * E], U8, name="x_in", align_bytes=64)
+            pieces = 2 if g == 0 else 1
+            width = TILES * E // pieces
+            for i in range(pieces):
+                cols = slice(width * i, width * (i + 1))
+                nc.sync.dma_start(out=tile[:, cols], in_=x_view[b, quarter][:, cols])
+            x_in[g] = tile
 
-        sc4 = keep.tile([P, 4], F32)
-        nc.scalar.dma_start(out=sc4[:], in_=x_scale.rearrange("o u (c p) -> p (o u c)", p=P))
-        bd_raw = keep.tile([P, 4], BF16)
-        nc.scalar.dma_start(out=bd_raw[:], in_=bq_d.rearrange("(p j) -> p j", j=4))
-        wd = keep.tile([P, 4 * E], BF16, align_bytes=64)
+        scale_cols = keep.tile([P, E // P], F32)
+        nc.scalar.dma_start(out=scale_cols[:], in_=x_scale.rearrange("o u (c p) -> p (o u c)", p=P))
+        bias_d_raw = keep.tile([P, 4], BF16)
+        nc.scalar.dma_start(out=bias_d_raw[:], in_=bq_d.rearrange("(p t) -> p t", t=4))
+        first_sine = keep.tile([P, 1], F32)
+        nc.scalar.activation(out=first_sine[:], in_=one[:], func=ACT.Sin)
+        bias_rows = keep.tile([P, P], BF16)
+        nc.vector.memset(bias_rows[:], 0.0)
         load_x(0)
-        nc.sync.dma_start(out=wd[:], in_=Wq_d.rearrange("(m t) k -> m (t k)", t=4))
+        w_down = keep.tile([P, 4 * E], BF16, align_bytes=64)
+        nc.sync.dma_start(out=w_down[:], in_=Wq_d.rearrange("(m t) k -> m (t k)", t=4))
         load_x(1)
-        b2_rows = keep.tile([P, P], BF16)
-        nc.vector.memset(b2_rows[:], 0.0)
-        w2 = keep.tile([P, 4, LAT], BF16, align_bytes=64)
-        for v, (w, bv) in enumerate(((Wq_u, bq_u), (Wrq, brq))):
+        w_up = keep.tile([P, 4, LAT], BF16, align_bytes=64)
+        for r, weight, bias in ((0, Wq_u, bq_u), (2, Wrq, brq)):
             nc.scalar.dma_start(
-                out=b2_rows[2 * v : 2 * v + 2, :].rearrange("s (h i) -> s h i", h=H),
-                in_=bv.rearrange("(h s i) -> s h i", h=H, s=2),
+                out=bias_rows[r : r + 2, :].rearrange("s (h i) -> s h i", h=H),
+                in_=bias.rearrange("(h s i) -> s h i", h=H, s=2),
             )
             for h in range(H):
                 nc.sync.dma_start(
-                    out=w2[32 * h : 32 * (h + 1), 2 * v : 2 * v + 2, :],
-                    in_=w.rearrange("(h s i) k -> h i s k", h=H, s=2)[h],
+                    out=w_up[FREQS * h : FREQS * (h + 1), r : r + 2, :],
+                    in_=weight.rearrange("(h s i) k -> h i s k", h=H, s=2)[h],
                 )
-        for g in range(2, 6):
+        for g in range(2, EARLY_LOADS):
             load_x(g)
 
+        freq = keep.tile([P, 1], F32)
+        quarter_start = keep.tile([P, 1], F32)
+        for quarter in range(QUARTERS):
+            rows = slice(FREQS * quarter, FREQS * (quarter + 1))
+            nc.gpsimd.iota(
+                freq[rows, :], pattern=[[0, 1]], base=0, channel_multiplier=1, allow_small_or_imprecise_dtypes=True
+            )
+            nc.vector.memset(quarter_start[rows, :], float(GROUP * quarter))
+        exponent = keep.tile([P, 1], F32)
+        nc.vector.tensor_scalar(out=exponent[:], in0=freq[:], scalar1=-1.0 / FREQS, scalar2=None, op0=ALU.mult)
+        off_diagonal = keep.tile([P, P], F32)
+        nc.gpsimd.iota(
+            off_diagonal[:], pattern=[[1, P]], base=0, channel_multiplier=-1, allow_small_or_imprecise_dtypes=True
+        )
+        power = keep.tile([P, 1], F32)
+        nc.gpsimd.tensor_tensor(out=power[:], in0=base[:], in1=exponent[:], op=ALU.pow)
+        place = keep.tile([P, TILES, P], F32)
+        nc.gpsimd.iota(
+            place[:],
+            pattern=[[1, TILES], [TILES, P]],
+            base=0,
+            channel_multiplier=0,
+            allow_small_or_imprecise_dtypes=True,
+        )
         ident = keep.tile([P, P], F32)
-        make_identity(nc, ident[:])
-        part = keep.tile([P, 1], F32)
-        nc.gpsimd.iota(part[:], pattern=[[0, 1]], base=0, channel_multiplier=1, allow_small_or_imprecise_dtypes=True)
-        base = keep.tile([P, 1], F32)
-        nc.gpsimd.memset(base[:], 10000.0)
-        pos = keep.tile([P, 4, P], F32)
-        nc.gpsimd.iota(pos[:], pattern=[[1, 4], [4, P]], base=0, channel_multiplier=0, allow_small_or_imprecise_dtypes=True)
-        GE = mybir.AluOpType.is_ge
-        jt = [keep.tile([P, 1], F32, name=f"jt{i}") for i in range(3)]
-        for i in range(3):
-            nc.vector.tensor_scalar(out=jt[i][:], in0=part[:], scalar1=32.0 * (i + 1), scalar2=float(GT), op0=GE, op1=MULT)
-        quarter = keep.tile([P, 1], F32)
-        nc.vector.tensor_tensor(out=jt[0][:], in0=jt[0][:], in1=jt[1][:], op=ADD)
-        nc.vector.tensor_tensor(out=quarter[:], in0=jt[0][:], in1=jt[2][:], op=ADD)
-        jm = keep.tile([P, 1], F32)
-        nc.vector.scalar_tensor_tensor(out=jm[:], in0=quarter[:], scalar=-32.0 / GT, in1=part[:], op0=MULT, op1=ADD)
-        jn = keep.tile([P, 1], F32)
-        nc.vector.tensor_scalar(out=jn[:], in0=jm[:], scalar1=-1.0 / 32, scalar2=None, op0=MULT)
-        wpow = keep.tile([P, 1], F32)
-        nc.gpsimd.tensor_tensor(out=wpow[:], in0=base[:], in1=jn[:], op=mybir.AluOpType.pow)
-        wcol = keep.tile([P, 1], F32)
-        nc.gpsimd.tensor_scalar(out=wcol[:], in0=wpow[:], scalar1=1 / (2 * math.pi), scalar2=0.0, op0=MULT, op1=ADD)
-        scratch = out[B - 1, S - GT : S].rearrange("(k r) h d -> k r (h d)", k=4)
-        tt = {k: keep.tile([P, GT], F32, name=f"tt_{k}") for k in ("t", "f", "u", "sn", "hs", "hh", "c", "smc", "mcs")}
-        tt_i = keep.tile([P, GT], I32)
-        tab = {k: keep.tile([P, CH, GT], F32, name=f"tab{k}") for k in (4, 2, 3)}
+        nc.vector.tensor_scalar(out=ident[:], in0=off_diagonal[:], scalar1=0.0, scalar2=None, op0=ALU.is_equal)
+        turns_per_place = keep.tile([P, 1], F32)
+        nc.vector.tensor_scalar(
+            out=turns_per_place[:], in0=power[:], scalar1=1 / (2 * math.pi), scalar2=None, op0=ALU.mult
+        )
+
+        made = {
+            name: keep.tile([P, GROUP], F32, name=f"made_{name}")
+            for name in ("turns", "whole", "part", "sine", "half_sine", "versine", "cos", "sin_less_cos", "less_both")
+        }
+        whole_turns = keep.tile([P, GROUP], I32)
 
         def angles():
             nc.vector.tensor_scalar(
-                out=tt["t"][:], in0=pos[:].rearrange("p a n -> p (a n)"), scalar1=quarter[:], scalar2=wcol[:], op0=ADD, op1=MULT
+                out=made["turns"][:],
+                in0=place[:].rearrange("p a n -> p (a n)"),
+                scalar1=quarter_start[:],
+                scalar2=turns_per_place[:],
+                op0=ALU.add,
+                op1=ALU.mult,
             )
-            nc.vector.tensor_copy(out=tt_i[:], in_=tt["t"][:])
-            nc.vector.tensor_copy(out=tt["f"][:], in_=tt_i[:])
-            nc.vector.tensor_tensor(out=tt["u"][:], in0=tt["t"][:], in1=tt["f"][:], op=SUB)
-            nc.scalar.activation(out=tt["hs"][:], in_=tt["u"][:], func=ACT.Sin, scale=math.pi)
-            nc.scalar.activation(out=tt["sn"][:], in_=tt["u"][:], func=ACT.Sin, scale=2 * math.pi)
+            nc.vector.tensor_copy(out=whole_turns[:], in_=made["turns"][:])
+            nc.vector.tensor_copy(out=made["whole"][:], in_=whole_turns[:])
+            nc.vector.tensor_tensor(out=made["part"][:], in0=made["turns"][:], in1=made["whole"][:], op=ALU.subtract)
+
+        def sines():
+            nc.scalar.activation(out=made["half_sine"][:], in_=made["part"][:], func=ACT.Sin, scale=math.pi)
+            nc.scalar.activation(out=made["sine"][:], in_=made["part"][:], func=ACT.Sin, scale=2 * math.pi)
+            nc.scalar.activation(
+                out=made["versine"][:], in_=made["half_sine"][:], func=ACT.Square, scale=math.sqrt(2)
+            )
+            nc.scalar.activation(
+                out=made["cos"][:], in_=made["versine"][:], func=ACT.Identity, scale=-1.0, bias=one[:]
+            )
+
+        table = {r: keep.tile([P, QUARTERS, GROUP], F32, name=f"table_{r}") for r in (SUM, 2, 3)}
 
         def tables():
-            STT = nc.vector.scalar_tensor_tensor
-            STT(out=tt["hh"][:], in0=tt["hs"][:], scalar=-2.0, in1=tt["hs"][:], op0=MULT, op1=MULT)
-            nc.vector.tensor_scalar(out=tt["c"][:], in0=tt["hh"][:], scalar1=1.0, scalar2=None, op0=ADD)
-            STT(out=tt["smc"][:], in0=tt["c"][:], scalar=-1.0, in1=tt["sn"][:], op0=MULT, op1=ADD)
-            STT(out=tt["mcs"][:], in0=tt["c"][:], scalar=-1.0, in1=tt["sn"][:], op0=MULT, op1=SUB)
-            src = {4: "c", 2: "smc", 3: "mcs"}
-            for i, k in enumerate((4, 2, 3)):
-                nc.sync.dma_start(out=scratch[i], in_=tt[src[k]][:])
-            for lo, hi in ((0, 1), (1, CH)):
-                for i, k in enumerate((4, 2, 3)):
+            stt = nc.vector.scalar_tensor_tensor
+            cos, sine = made["cos"][:], made["sine"][:]
+            stt(out=made["sin_less_cos"][:], in0=cos, scalar=-1.0, in1=sine, op0=ALU.mult, op1=ALU.add)
+            stt(out=made["less_both"][:], in0=cos, scalar=-1.0, in1=sine, op0=ALU.mult, op1=ALU.subtract)
+            parked = out[B - 1, S - GROUP : S].rearrange("(i r) h d -> i r (h d)", i=TILES)
+            sources = ((SUM, "cos"), (2, "sin_less_cos"), (3, "less_both"))
+            for i, (r, name) in enumerate(sources):
+                nc.sync.dma_start(out=parked[i], in_=made[name][:])
+            for lo, hi in ((0, 1), (1, QUARTERS)):
+                for i, (r, name) in enumerate(sources):
                     for h in range(H):
                         nc.sync.dma_start(
-                            out=tab[k][32 * h : 32 * (h + 1), lo:hi, :],
-                            in_=scratch[i][32 * lo : 32 * hi, :].rearrange("(c j) n -> j c n", j=32),
+                            out=table[r][FREQS * h : FREQS * (h + 1), lo:hi, :],
+                            in_=parked[i][FREQS * lo : FREQS * hi, :].rearrange("(q j) n -> j q n", j=FREQS),
                         )
 
-        def turn_half(words2, step8, xt):
+        def turn_half(pairs, bank):
             for a in range(2):
                 for u in range(2):
-                    blk = words2[:, 256 * a : 256 * (a + 1)]
-                    if step8:
-                        src = blk.rearrange("p (q u i) -> p u q i", u=2, i=8)[:, u]
-                    else:
-                        src = blk[:, u::2]
-                    nc.tensor.transpose(xt[:, a, u, :], src, ident[:])
+                    nc.tensor.transpose(bank[:, a, u, :], pairs[:, E // 2 * a + u : E // 2 * (a + 1) : 2], ident[:])
 
-        def turn_out(grouped, i, xt):
+        def empty_half(k_major, i, bank):
             nc.scalar.copy(
-                out=grouped[:].bitcast(F32)[:, 512 * i : 512 * (i + 1)].rearrange("p (a n u) -> p a n u", a=2, u=2),
-                in_=xt[:].rearrange("p a u n -> p a n u"),
+                out=k_major[:].bitcast(F32)[:, E * i : E * (i + 1)].rearrange("p (a n u) -> p a n u", a=2, u=2),
+                in_=bank[:].rearrange("p a u n -> p a n u"),
             )
 
-        def quant(grouped, pool, name, bufs):
-            codes = pool.tile([P, GT], U32, name=name + "_c", align_bytes=64, bufs=bufs)
-            scales = pool.tile([P, GT], U8, name=name + "_s", align_bytes=64, bufs=bufs)
-            nc.vector.quantize_mx(out=codes[:].bitcast(FP8X4), scales=scales[:], in_=grouped[:])
-            return codes, scales
+        def quantise(k_major, pool, name, bufs):
+            codes = pool.tile([P, GROUP], U32, name=name + "_codes", align_bytes=64, bufs=bufs)
+            scales = pool.tile([P, GROUP], U8, name=name + "_scales", align_bytes=64, bufs=bufs)
+            nc.vector.quantize_mx(out=codes[:].bitcast(FP8X4), scales=scales[:], in_=k_major[:])
+            return codes[:], scales[:]
 
-        def mx(ps, w, m, r, start=True, stop=True):
+        def multiply(bank, weight, m, moving, start=True, stop=True):
+            cols = slice(m * P, (m + 1) * P)
             nc.tensor.matmul_mx(
-                out=ps[:],
-                lhsT=w[0][:, m * P : (m + 1) * P].bitcast(FP8X4),
-                lhsT_scale=w[1][:, m * P : (m + 1) * P],
-                rhs=r[0][:].bitcast(FP8X4),
-                rhs_scale=r[1][:],
+                out=bank,
+                lhsT=weight[0][:, cols].bitcast(FP8X4),
+                lhsT_scale=weight[1][:, cols],
+                rhs=moving[0].bitcast(FP8X4),
+                rhs_scale=moving[1],
                 start=start,
                 stop=stop,
             )
 
-        def weights(src, step8, name):
-            wg = work.tile([P, 4 * E], BF16, name="xg", align_bytes=64, bufs=3)
+        scale_bank = psum.tile([P, 2, 2, P], F32, name="x_bank")
+        for c in range(E // P):
+            nc.tensor.transpose(
+                scale_bank[:, c // 2, c % 2, :], scale_cols[:, c : c + 1].to_broadcast([P, P]), ident[:]
+            )
+        x_scales = keep.tile([P, 2 * E], F32, align_bytes=64)
+        for i in range(2):
+            nc.scalar.copy(out=x_scales[:, E * i : E * (i + 1)], in_=scale_bank[:].rearrange("p a u n -> p (a u n)"))
+
+        bias_d = keep.tile([P, 4], F32)
+        nc.vector.tensor_copy(out=bias_d[:], in_=bias_d_raw[:])
+        bias_up = keep.tile([P, 5], F32)
+        weights = {}
+
+        def turn_weights(rows, name):
+            weights[name] = work.tile([P, 4 * E], BF16, name="x_k_major", align_bytes=64, bufs=3)
             for i in range(2):
-                xt = psum.tile([P, 2, 2, P], F32, name="xt")
-                turn_half(src.bitcast(F32)[:, 512 * i : 512 * (i + 1)], step8, xt)
-                turn_out(wg, i, xt)
-            return quant(wg, keep, name, 1)
+                bank = psum.tile([P, 2, 2, P], F32, name="x_bank")
+                turn_half(rows.bitcast(F32)[:, E * i : E * (i + 1)], bank)
+                empty_half(weights[name], i, bank)
 
-        scp = psum.tile([P, 2, 2, P], F32, name="xt")
-        for c in range(4):
-            nc.tensor.transpose(scp[:, c // 2, c % 2, :], sc4[:, c : c + 1].to_broadcast([P, P]), ident[:])
-        sc = keep.tile([P, 2 * E], F32, align_bytes=64)
-        for r in range(2):
-            nc.scalar.copy(out=sc[:, r * E : (r + 1) * E], in_=scp[:].rearrange("p a u n -> p (a u n)"))
+        def quantise_weights(name):
+            weights[name] = quantise(weights[name], keep, name, 1)
 
-        bd = keep.tile([P, 4], F32)
-        nc.vector.tensor_copy(out=bd[:], in_=bd_raw[:])
-        b2 = keep.tile([P, 5], F32)
-        wts = {}
-
-        def prep2():
-            ident_b = keep.tile([P, P], BF16)
-            nc.vector.tensor_copy(out=ident_b[:], in_=ident[:])
-            bps = psum.tile([P, P], BF16, name="ot")
-            nc.tensor.transpose(bps[:], b2_rows[:], ident_b[:])
-            nc.vector.tensor_copy(out=b2[:, 0:4], in_=bps[:, 0:4])
-            wts["w2"] = weights(w2[:].rearrange("p m k -> p (m k)"), False, "w2")
-            nc.vector.tensor_tensor(out=b2[:, 4:5], in0=b2[:, 2:3], in1=b2[:, 3:4], op=ADD)
-
-        xs, xt, xg, xq, s1, qp, qi, qq, s2, q1, km, ot, o_sb = ({} for i in range(13))
-
-        def f_TT(g, i):
-            xs[g, i] = work.tile([P, 2 * E], BF16, name="xs", align_bytes=64, bufs=4)
+        def prepare_up():
+            ident_bf16 = keep.tile([P, P], BF16)
+            nc.vector.tensor_copy(out=ident_bf16[:], in_=ident[:])
+            bias_bank = psum.tile([P, P], BF16, name="out_bank")
+            nc.tensor.transpose(bias_bank[:], bias_rows[:], ident_bf16[:])
+            nc.vector.tensor_copy(out=bias_up[:, 0:4], in_=bias_bank[:, 0:4])
+            turn_weights(w_up[:].rearrange("p r k -> p (r k)"), "up")
+            quantise_weights("up")
             nc.vector.tensor_tensor(
-                out=xs[g, i][:], in0=xb[g][:, 1024 * i : 1024 * (i + 1)].bitcast(FP8), in1=sc[:], op=MULT
+                out=bias_up[:, SUM : SUM + 1], in0=bias_up[:, 2:3], in1=bias_up[:, 3:4], op=ALU.add
             )
 
-        def f_X(g, i):
-            xt[g, i] = psum.tile([P, 2, 2, P], F32, name="xt")
-            turn_half(xs[g, i][:].bitcast(F32), False, xt[g, i])
+        x_scaled, x_banks, x_k_major, x_mx = {}, {}, {}, {}
+        d_banks, d_outputs, q_k_major, q_mx = {}, {}, {}, {}
+        up_banks, q1, products, out_banks, result, tiles_done = {}, {}, {}, {}, {}, {}
 
-        def f_xe(g, i):
-            if i == 0:
-                xg[g] = work.tile([P, 4 * E], BF16, name="xg", align_bytes=64, bufs=3)
-            turn_out(xg[g], i, xt[g, i])
+        def scale_x(g, i):
+            x_scaled[g, i] = work.tile([P, 2 * E], BF16, name="x_scaled", align_bytes=64, bufs=6)
+            width = E if g == 0 else 2 * E
+            for lo in range(0, 2 * E, width):
+                nc.vector.tensor_tensor(
+                    out=x_scaled[g, i][:, lo : lo + width],
+                    in0=x_in[g][:, 2 * E * i + lo : 2 * E * i + lo + width].bitcast(FP8),
+                    in1=x_scales[:, :width],
+                    op=ALU.mult,
+                )
 
-        def f_qx(g):
-            xq[g] = quant(xg[g], work, "xq", 3)
+        def turn_x(g, i):
+            x_banks[g, i] = psum.tile([P, 2, 2, P], F32, name="x_bank")
+            turn_half(x_scaled[g, i][:].bitcast(F32), x_banks[g, i])
 
-        def f_A(g, j):
-            s1[g, j] = psum.tile([P, GT], F32, name="s1")
-            mx(s1[g, j], wts["wd"], j, xq[g])
+        def empty_x(g, i):
+            if g not in x_k_major:
+                x_k_major[g] = work.tile([P, 4 * E], BF16, name="x_k_major", align_bytes=64, bufs=3)
+            empty_half(x_k_major[g], i, x_banks[g, i])
 
-        def f_p(g, j):
-            if j == 0:
-                qp[g] = work.tile([P, 4, GT], BF16, name="qp", align_bytes=64)
-            nc.scalar.activation(out=qp[g][:, j, :], in_=s1[g, j][:], func=ACT.Identity, bias=bd[:, j : j + 1])
+        def quantise_x(g):
+            x_mx[g] = quantise(x_k_major[g], work, "x_mx", 3)
 
-        def f_I(g):
-            qi[g] = work.tile([P, 4 * GT], BF16, name="qi", align_bytes=64)
+        def down(g, j):
+            d_banks[g, j] = psum.tile([P, 4, P], F32, name="d_bank")
+            if g in DIRECT:
+                tokens = slice(j * P, (j + 1) * P)
+                for t in range(4):
+                    multiply(d_banks[g, j][:, t, :], weights["down"], t, [operand[:, tokens] for operand in x_mx[g]])
+            else:
+                multiply(d_banks[g, j][:].rearrange("p t n -> p (t n)"), weights["down"], j, x_mx[g])
+
+        def latent(g, j):
+            if g in DIRECT:
+                if g not in q_k_major:
+                    q_k_major[g] = work.tile([P, 4 * GROUP], BF16, name="q_k_major", align_bytes=64)
+                nc.vector.tensor_tensor(
+                    out=q_k_major[g][:, GROUP * j : GROUP * (j + 1)].rearrange("p (n t) -> p n t", t=4),
+                    in0=d_banks[g, j][:].rearrange("p t n -> p n t"),
+                    in1=bias_d[:].unsqueeze(1).to_broadcast([P, P, 4]),
+                    op=ALU.add,
+                )
+                return
+            if g not in d_outputs:
+                d_outputs[g] = work.tile([P, 4, GROUP], BF16, name="d_outputs", align_bytes=64)
+            nc.scalar.activation(
+                out=d_outputs[g][:, j, :],
+                in_=d_banks[g, j][:].rearrange("p t n -> p (t n)"),
+                func=ACT.Identity,
+                bias=bias_d[:, j : j + 1],
+            )
+
+        def interleave(g):
+            if g in DIRECT:
+                return
+            q_k_major[g] = work.tile([P, 4 * GROUP], BF16, name="q_k_major", align_bytes=64)
             nc.vector.tensor_copy(
-                out=qi[g][:].rearrange("p (c i t) -> p c t i", i=4, t=4), in_=qp[g][:].rearrange("p t (c i) -> p c t i", i=4)
+                out=q_k_major[g][:].rearrange("p (c i t) -> p c t i", i=4, t=4),
+                in_=d_outputs[g][:].rearrange("p t (c i) -> p c t i", i=4),
             )
 
-        def f_qq(g):
-            qq[g] = quant(qi[g], work, "qq", 2)
+        def quantise_q(g):
+            q_mx[g] = quantise(q_k_major[g], work, "q_mx", 2)
 
-        def f_C(g, k):
-            s2[g, k] = psum.tile([P, GT], F32, name="s2")
-            if k < 4:
-                mx(s2[g, k], wts["w2"], k, qq[g])
+        def up(g, r):
+            up_banks[g, r] = psum.tile([P, GROUP], F32, name="up_bank")
+            if r == SUM:
+                multiply(up_banks[g, r][:], weights["up"], 2, q_mx[g], stop=False)
+                multiply(up_banks[g, r][:], weights["up"], 3, q_mx[g], start=False)
             else:
-                mx(s2[g, k], wts["w2"], 2, qq[g], stop=False)
-                mx(s2[g, k], wts["w2"], 3, qq[g], start=False)
+                multiply(up_banks[g, r][:], weights["up"], r, q_mx[g])
 
-        def f_q(g, k):
-            q1[g, k] = work.tile([P, GT], F32, name="q1", bufs=4)
-            nc.scalar.activation(out=q1[g, k][:], in_=s2[g, k][:], func=ACT.Identity, bias=b2[:, k : k + 1])
+        def bias_q1(g, r):
+            q1[g, r] = work.tile([P, GROUP], F32, name="q1", bufs=4)
+            nc.scalar.activation(
+                out=q1[g, r][:], in_=up_banks[g, r][:], func=ACT.Identity, bias=bias_up[:, r : r + 1]
+            )
 
-        def f_T(g, k, unused):
-            km[g, k] = work.tile([P, GT], F32, name="km", bufs=8)
+        def rotate(g, r):
+            products[g, r] = work.tile([P, GROUP], F32, name="products", bufs=8)
             nc.vector.scalar_tensor_tensor(
-                out=km[g, k][:], in0=s2[g, k][:], scalar=b2[:, k : k + 1], in1=tab[k][:, groups[g][0], :], op0=ADD, op1=MULT
+                out=products[g, r][:],
+                in0=up_banks[g, r][:],
+                scalar=bias_up[:, r : r + 1],
+                in1=table[r][:, GROUPS[g][0], :],
+                op0=ALU.add,
+                op1=ALU.mult,
             )
 
-        def f_O(g, a):
-            cols = slice(a * P, (a + 1) * P)
-            t = psum.tile([P, 4, P], F32, name="ot")
-            for k in range(2):
-                nc.tensor.transpose(t[:, k, :], q1[g, k][:, cols], ident[:])
-            for k in (2, 3):
-                nc.tensor.matmul(t[:, k, :], lhsT=km[g, 4][:, cols], rhs=ident[:], start=True, stop=False, is_transpose=True)
-                nc.tensor.matmul(t[:, k, :], lhsT=km[g, 5 - k][:, cols], rhs=ident[:], start=False, stop=True, is_transpose=True)
-            ot[g, a] = t
+        def turn_back(g, a):
+            tokens = slice(a * P, (a + 1) * P)
+            bank = psum.tile([P, 4, P], F32, name="out_bank")
+            for r in range(2):
+                nc.tensor.transpose(bank[:, r, :], q1[g, r][:, tokens], ident[:])
+            for r, other in ((2, 3), (3, 2)):
+                for addend, first in ((SUM, True), (other, False)):
+                    nc.tensor.matmul(
+                        bank[:, r, :],
+                        lhsT=products[g, addend][:, tokens],
+                        rhs=ident[:],
+                        start=first,
+                        stop=not first,
+                        is_transpose=True,
+                    )
+            out_banks[g, a] = bank
 
-        done = {}
-
-        def f_o(g, a):
-            if g not in o_sb:
-                o_sb[g] = work.tile([P, 4, E], F32, name="o_sb", bufs=3)
-                done[g] = 0
-            src = ot[g, a][:].rearrange("p t (h i) -> p h t i", h=H)
-            dst = o_sb[g][:, a, :].rearrange("p (h t i) -> p h t i", h=H, t=4)
-            if a == 3 and g % 4 < 2:
-                nc.vector.tensor_copy(out=dst, in_=src)
+        def store(g, a):
+            last = g == len(GROUPS) - 1
+            if g not in result:
+                result[g] = work.tile([P, TILES, E], F32, name="result", bufs=3)
+                tiles_done[g] = 0
+            source = out_banks[g, a][:].rearrange("p r (h i) -> p h r i", h=H)
+            target = result[g][:, a, :].rearrange("p (h r i) -> p h r i", h=H, r=4)
+            if (a == TILES - 1 and g % 4 < 2) or (last and a % 2 == 1):
+                nc.vector.tensor_copy(out=target, in_=source)
             else:
-                nc.scalar.copy(out=dst, in_=src)
-            done[g] += 1
-            if done[g] == 4:
-                c, b = groups[g]
-                nc.sync.dma_start(out=out_view[b, c], in_=o_sb[g][:].rearrange("p a f -> p (a f)"))
+                nc.scalar.copy(out=target, in_=source)
+            tiles_done[g] += 1
+            quarter, b = GROUPS[g]
+            if last:
+                nc.sync.dma_start(out=out_view[b, quarter][:, E * a : E * (a + 1)], in_=result[g][:, a, :])
+            elif tiles_done[g] == TILES:
+                nc.sync.dma_start(out=out_view[b, quarter], in_=result[g][:].rearrange("p a f -> p (a f)"))
 
-        steps = {"TT": f_TT, "X": f_X, "xe": f_xe, "qx": f_qx, "A": f_A, "p": f_p, "I": f_I, "qq": f_qq, "C": f_C, "q": f_q, "T": f_T, "O": f_O, "o": f_o}
+        stages = {
+            "scale_x": scale_x,
+            "turn_x": turn_x,
+            "empty_x": empty_x,
+            "quantise_x": quantise_x,
+            "down": down,
+            "latent": latent,
+            "interleave": interleave,
+            "quantise_q": quantise_q,
+            "up": up,
+            "bias_q1": bias_q1,
+            "rotate": rotate,
+            "turn_back": turn_back,
+            "store": store,
+        }
 
+        one_time = {
+            -2: [lambda: turn_weights(w_down[:], "down")],
+            0: [sines, lambda: quantise_weights("down")],
+            1: [tables, lambda: [load_x(g) for g in range(EARLY_LOADS, len(GROUPS))]],
+            2: [prepare_up],
+        }
         angles()
-        wts["wd"] = weights(wd[:], False, "wd")
-        for s in range(-3, n + 7):
-            if s == 0:
-                tables()
-                for g in range(6, n):
-                    load_x(g)
-            if s == 1:
-                prep2()
+        for step in range(min(min(LAGS), *one_time), len(GROUPS) + max(LAGS)):
+            for job in one_time.get(step, []):
+                job()
             for name, lag, *args in ORDER:
-                g = s - lag
-                if 0 <= g < n:
-                    steps[name](g, *args)
+                g = step - lag
+                if 0 <= g < len(GROUPS):
+                    stages[name](g, *args)

import math
from contextlib import ExitStack

import concourse.mybir as mybir

F32 = mybir.dt.float32
BF16 = mybir.dt.bfloat16
I32 = mybir.dt.int32
U32 = mybir.dt.uint32
U8 = mybir.dt.uint8
FP8 = mybir.dt.float8_e4m3fn
FP8X4 = mybir.dt.float8_e4m3fn_x4
ALU = mybir.AluOpType
ACT = mybir.ActivationFunctionType

P = 128
B, S, E, LAT, H = 4, 2048, 512, 512, 4
FREQS = 32
GROUP = 512
TILES = GROUP // P
QUARTERS = S // GROUP
GROUPS = [(quarter, b) for quarter in range(QUARTERS) for b in range(B)]
SUM = 4
FLOPS = 2 * B * S * LAT * (E + H * 2 * 2 * FREQS)

EARLY_LOADS = 6

DIRECT = (14, 15)

ORDER = (
    ("down", 2, 1),
    ("latent", 2, 1),
    ("down", 2, 0),
    ("latent", 2, 0),
    ("turn_back", 4, 0),
    ("up", 3, 0),
    ("quantise_x", 1),
    ("bias_q1", 3, 0),
    ("store", 4, 0),
    ("up", 3, 4),
    ("down", 2, 2),
    ("turn_back", 4, 1),
    ("rotate", 3, 4),
    ("down", 2, 3),
    ("up", 3, 3),
    ("latent", 2, 2),
    ("rotate", 3, 3),
    ("latent", 2, 3),
    ("turn_x", 0, 0),
    ("interleave", 2),
    ("turn_back", 4, 2),
    ("store", 4, 1),
    ("turn_x", 0, 1),
    ("empty_x", 0, 0),
    ("up", 3, 1),
    ("store", 4, 2),
    ("up", 3, 2),
    ("rotate", 3, 2),
    ("bias_q1", 3, 1),
    ("turn_back", 4, 3),
    ("empty_x", 0, 1),
    ("quantise_q", 2),
    ("store", 4, 3),
    ("scale_x", -1, 0),
    ("scale_x", -1, 1),
)
LAGS = [item[1] for item in ORDER]


def tile_multiheadlatentattention_pa_t_kernel(
    tc, x_bytes, x_scale, Wq_d, bq_d, Wq_u, bq_u, Wrq, brq, out
):
    nc = tc.nc
    with ExitStack() as ctx:
        keep = ctx.enter_context(tc.tile_pool(name="keep", bufs=1))
        bytes_in = ctx.enter_context(tc.tile_pool(name="bytes_in", bufs=len(GROUPS)))
        work = ctx.enter_context(tc.tile_pool(name="work", bufs=2))
        psum = ctx.enter_context(tc.psum_pool(name="psum", bufs=2))
        ctx.enter_context(tc.manual_schedule())

        one = keep.tile([P, 1], F32)
        nc.vector.memset(one[:], 1.0)
        base = keep.tile([P, 1], F32)
        nc.vector.memset(base[:], 10000.0)

        x_view = x_bytes.rearrange("b (q p a) k -> b q p (a k)", q=QUARTERS, a=TILES)
        out_view = out.rearrange("b (q p a) h d -> b q p (a h d)", q=QUARTERS, a=TILES)
        x_in = {}

        def load_x(g):
            quarter, b = GROUPS[g]
            tile = bytes_in.tile([P, TILES * E], U8, name="x_in", align_bytes=64)
            pieces = 2 if g == 0 else 1
            width = TILES * E // pieces
            for i in range(pieces):
                cols = slice(width * i, width * (i + 1))
                nc.sync.dma_start(out=tile[:, cols], in_=x_view[b, quarter][:, cols])
            x_in[g] = tile

        scale_cols = keep.tile([P, E // P], F32)
        nc.scalar.dma_start(out=scale_cols[:], in_=x_scale.rearrange("o u (c p) -> p (o u c)", p=P))
        bias_d_raw = keep.tile([P, 4], BF16)
        nc.scalar.dma_start(out=bias_d_raw[:], in_=bq_d.rearrange("(p t) -> p t", t=4))
        first_sine = keep.tile([P, 1], F32)
        nc.scalar.activation(out=first_sine[:], in_=one[:], func=ACT.Sin)
        bias_rows = keep.tile([P, P], BF16)
        nc.vector.memset(bias_rows[:], 0.0)
        load_x(0)
        w_down = keep.tile([P, 4 * E], BF16, align_bytes=64)
        nc.sync.dma_start(out=w_down[:], in_=Wq_d.rearrange("(m t) k -> m (t k)", t=4))
        load_x(1)
        w_up = keep.tile([P, 4, LAT], BF16, align_bytes=64)
        for r, weight, bias in ((0, Wq_u, bq_u), (2, Wrq, brq)):
            nc.scalar.dma_start(
                out=bias_rows[r : r + 2, :].rearrange("s (h i) -> s h i", h=H),
                in_=bias.rearrange("(h s i) -> s h i", h=H, s=2),
            )
            for h in range(H):
                nc.sync.dma_start(
                    out=w_up[FREQS * h : FREQS * (h + 1), r : r + 2, :],
                    in_=weight.rearrange("(h s i) k -> h i s k", h=H, s=2)[h],
                )
        for g in range(2, EARLY_LOADS):
            load_x(g)

        freq = keep.tile([P, 1], F32)
        quarter_start = keep.tile([P, 1], F32)
        for quarter in range(QUARTERS):
            rows = slice(FREQS * quarter, FREQS * (quarter + 1))
            nc.gpsimd.iota(
                freq[rows, :], pattern=[[0, 1]], base=0, channel_multiplier=1, allow_small_or_imprecise_dtypes=True
            )
            nc.vector.memset(quarter_start[rows, :], float(GROUP * quarter))
        exponent = keep.tile([P, 1], F32)
        nc.vector.tensor_scalar(out=exponent[:], in0=freq[:], scalar1=-1.0 / FREQS, scalar2=None, op0=ALU.mult)
        off_diagonal = keep.tile([P, P], F32)
        nc.gpsimd.iota(
            off_diagonal[:], pattern=[[1, P]], base=0, channel_multiplier=-1, allow_small_or_imprecise_dtypes=True
        )
        power = keep.tile([P, 1], F32)
        nc.gpsimd.tensor_tensor(out=power[:], in0=base[:], in1=exponent[:], op=ALU.pow)
        place = keep.tile([P, TILES, P], F32)
        nc.gpsimd.iota(
            place[:],
            pattern=[[1, TILES], [TILES, P]],
            base=0,
            channel_multiplier=0,
            allow_small_or_imprecise_dtypes=True,
        )
        ident = keep.tile([P, P], F32)
        nc.vector.tensor_scalar(out=ident[:], in0=off_diagonal[:], scalar1=0.0, scalar2=None, op0=ALU.is_equal)
        turns_per_place = keep.tile([P, 1], F32)
        nc.vector.tensor_scalar(
            out=turns_per_place[:], in0=power[:], scalar1=1 / (2 * math.pi), scalar2=None, op0=ALU.mult
        )

        made = {
            name: keep.tile([P, GROUP], F32, name=f"made_{name}")
            for name in ("turns", "whole", "part", "sine", "half_sine", "versine", "cos", "sin_less_cos", "less_both")
        }
        whole_turns = keep.tile([P, GROUP], I32)

        def angles():
            nc.vector.tensor_scalar(
                out=made["turns"][:],
                in0=place[:].rearrange("p a n -> p (a n)"),
                scalar1=quarter_start[:],
                scalar2=turns_per_place[:],
                op0=ALU.add,
                op1=ALU.mult,
            )
            nc.vector.tensor_copy(out=whole_turns[:], in_=made["turns"][:])
            nc.vector.tensor_copy(out=made["whole"][:], in_=whole_turns[:])
            nc.vector.tensor_tensor(out=made["part"][:], in0=made["turns"][:], in1=made["whole"][:], op=ALU.subtract)

        def sines():
            nc.scalar.activation(out=made["half_sine"][:], in_=made["part"][:], func=ACT.Sin, scale=math.pi)
            nc.scalar.activation(out=made["sine"][:], in_=made["part"][:], func=ACT.Sin, scale=2 * math.pi)
            nc.scalar.activation(
                out=made["versine"][:], in_=made["half_sine"][:], func=ACT.Square, scale=math.sqrt(2)
            )
            nc.scalar.activation(
                out=made["cos"][:], in_=made["versine"][:], func=ACT.Identity, scale=-1.0, bias=one[:]
            )

        table = {r: keep.tile([P, QUARTERS, GROUP], F32, name=f"table_{r}") for r in (SUM, 2, 3)}

        def tables():
            stt = nc.vector.scalar_tensor_tensor
            cos, sine = made["cos"][:], made["sine"][:]
            stt(out=made["sin_less_cos"][:], in0=cos, scalar=-1.0, in1=sine, op0=ALU.mult, op1=ALU.add)
            stt(out=made["less_both"][:], in0=cos, scalar=-1.0, in1=sine, op0=ALU.mult, op1=ALU.subtract)
            parked = out[B - 1, S - GROUP : S].rearrange("(i r) h d -> i r (h d)", i=TILES)
            sources = ((SUM, "cos"), (2, "sin_less_cos"), (3, "less_both"))
            for i, (r, name) in enumerate(sources):
                nc.sync.dma_start(out=parked[i], in_=made[name][:])
            for lo, hi in ((0, 1), (1, QUARTERS)):
                for i, (r, name) in enumerate(sources):
                    for h in range(H):
                        nc.sync.dma_start(
                            out=table[r][FREQS * h : FREQS * (h + 1), lo:hi, :],
                            in_=parked[i][FREQS * lo : FREQS * hi, :].rearrange("(q j) n -> j q n", j=FREQS),
                        )

        def turn_half(pairs, bank):
            for a in range(2):
                for u in range(2):
                    nc.tensor.transpose(bank[:, a, u, :], pairs[:, E // 2 * a + u : E // 2 * (a + 1) : 2], ident[:])

        def empty_half(k_major, i, bank):
            nc.scalar.copy(
                out=k_major[:].bitcast(F32)[:, E * i : E * (i + 1)].rearrange("p (a n u) -> p a n u", a=2, u=2),
                in_=bank[:].rearrange("p a u n -> p a n u"),
            )

        def quantise(k_major, pool, name, bufs):
            codes = pool.tile([P, GROUP], U32, name=name + "_codes", align_bytes=64, bufs=bufs)
            scales = pool.tile([P, GROUP], U8, name=name + "_scales", align_bytes=64, bufs=bufs)
            nc.vector.quantize_mx(out=codes[:].bitcast(FP8X4), scales=scales[:], in_=k_major[:])
            return codes[:], scales[:]

        def multiply(bank, weight, m, moving, start=True, stop=True):
            cols = slice(m * P, (m + 1) * P)
            nc.tensor.matmul_mx(
                out=bank,
                lhsT=weight[0][:, cols].bitcast(FP8X4),
                lhsT_scale=weight[1][:, cols],
                rhs=moving[0].bitcast(FP8X4),
                rhs_scale=moving[1],
                start=start,
                stop=stop,
            )

        scale_bank = psum.tile([P, 2, 2, P], F32, name="x_bank")
        for c in range(E // P):
            nc.tensor.transpose(
                scale_bank[:, c // 2, c % 2, :], scale_cols[:, c : c + 1].to_broadcast([P, P]), ident[:]
            )
        x_scales = keep.tile([P, 2 * E], F32, align_bytes=64)
        for i in range(2):
            nc.scalar.copy(out=x_scales[:, E * i : E * (i + 1)], in_=scale_bank[:].rearrange("p a u n -> p (a u n)"))

        bias_d = keep.tile([P, 4], F32)
        nc.vector.tensor_copy(out=bias_d[:], in_=bias_d_raw[:])
        bias_up = keep.tile([P, 5], F32)
        weights = {}

        def turn_weights(rows, name):
            weights[name] = work.tile([P, 4 * E], BF16, name="x_k_major", align_bytes=64, bufs=3)
            for i in range(2):
                bank = psum.tile([P, 2, 2, P], F32, name="x_bank")
                turn_half(rows.bitcast(F32)[:, E * i : E * (i + 1)], bank)
                empty_half(weights[name], i, bank)

        def quantise_weights(name):
            weights[name] = quantise(weights[name], keep, name, 1)

        def prepare_up():
            ident_bf16 = keep.tile([P, P], BF16)
            nc.vector.tensor_copy(out=ident_bf16[:], in_=ident[:])
            bias_bank = psum.tile([P, P], BF16, name="out_bank")
            nc.tensor.transpose(bias_bank[:], bias_rows[:], ident_bf16[:])
            nc.vector.tensor_copy(out=bias_up[:, 0:4], in_=bias_bank[:, 0:4])
            turn_weights(w_up[:].rearrange("p r k -> p (r k)"), "up")
            quantise_weights("up")
            nc.vector.tensor_tensor(
                out=bias_up[:, SUM : SUM + 1], in0=bias_up[:, 2:3], in1=bias_up[:, 3:4], op=ALU.add
            )

        x_scaled, x_banks, x_k_major, x_mx = {}, {}, {}, {}
        d_banks, d_outputs, q_k_major, q_mx = {}, {}, {}, {}
        up_banks, q1, products, out_banks, result, tiles_done = {}, {}, {}, {}, {}, {}

        def scale_x(g, i):
            x_scaled[g, i] = work.tile([P, 2 * E], BF16, name="x_scaled", align_bytes=64, bufs=6)
            width = E if g == 0 else 2 * E
            for lo in range(0, 2 * E, width):
                nc.vector.tensor_tensor(
                    out=x_scaled[g, i][:, lo : lo + width],
                    in0=x_in[g][:, 2 * E * i + lo : 2 * E * i + lo + width].bitcast(FP8),
                    in1=x_scales[:, :width],
                    op=ALU.mult,
                )

        def turn_x(g, i):
            x_banks[g, i] = psum.tile([P, 2, 2, P], F32, name="x_bank")
            turn_half(x_scaled[g, i][:].bitcast(F32), x_banks[g, i])

        def empty_x(g, i):
            if g not in x_k_major:
                x_k_major[g] = work.tile([P, 4 * E], BF16, name="x_k_major", align_bytes=64, bufs=3)
            empty_half(x_k_major[g], i, x_banks[g, i])

        def quantise_x(g):
            x_mx[g] = quantise(x_k_major[g], work, "x_mx", 3)

        def down(g, j):
            d_banks[g, j] = psum.tile([P, 4, P], F32, name="d_bank")
            if g in DIRECT:
                tokens = slice(j * P, (j + 1) * P)
                for t in range(4):
                    multiply(d_banks[g, j][:, t, :], weights["down"], t, [operand[:, tokens] for operand in x_mx[g]])
            else:
                multiply(d_banks[g, j][:].rearrange("p t n -> p (t n)"), weights["down"], j, x_mx[g])

        def latent(g, j):
            if g in DIRECT:
                if g not in q_k_major:
                    q_k_major[g] = work.tile([P, 4 * GROUP], BF16, name="q_k_major", align_bytes=64)
                nc.vector.tensor_tensor(
                    out=q_k_major[g][:, GROUP * j : GROUP * (j + 1)].rearrange("p (n t) -> p n t", t=4),
                    in0=d_banks[g, j][:].rearrange("p t n -> p n t"),
                    in1=bias_d[:].unsqueeze(1).to_broadcast([P, P, 4]),
                    op=ALU.add,
                )
                return
            if g not in d_outputs:
                d_outputs[g] = work.tile([P, 4, GROUP], BF16, name="d_outputs", align_bytes=64)
            nc.scalar.activation(
                out=d_outputs[g][:, j, :],
                in_=d_banks[g, j][:].rearrange("p t n -> p (t n)"),
                func=ACT.Identity,
                bias=bias_d[:, j : j + 1],
            )

        def interleave(g):
            if g in DIRECT:
                return
            q_k_major[g] = work.tile([P, 4 * GROUP], BF16, name="q_k_major", align_bytes=64)
            nc.vector.tensor_copy(
                out=q_k_major[g][:].rearrange("p (c i t) -> p c t i", i=4, t=4),
                in_=d_outputs[g][:].rearrange("p t (c i) -> p c t i", i=4),
            )

        def quantise_q(g):
            q_mx[g] = quantise(q_k_major[g], work, "q_mx", 2)

        def up(g, r):
            up_banks[g, r] = psum.tile([P, GROUP], F32, name="up_bank")
            if r == SUM:
                multiply(up_banks[g, r][:], weights["up"], 2, q_mx[g], stop=False)
                multiply(up_banks[g, r][:], weights["up"], 3, q_mx[g], start=False)
            else:
                multiply(up_banks[g, r][:], weights["up"], r, q_mx[g])

        def bias_q1(g, r):
            q1[g, r] = work.tile([P, GROUP], F32, name="q1", bufs=4)
            nc.scalar.activation(
                out=q1[g, r][:], in_=up_banks[g, r][:], func=ACT.Identity, bias=bias_up[:, r : r + 1]
            )

        def rotate(g, r):
            products[g, r] = work.tile([P, GROUP], F32, name="products", bufs=8)
            nc.vector.scalar_tensor_tensor(
                out=products[g, r][:],
                in0=up_banks[g, r][:],
                scalar=bias_up[:, r : r + 1],
                in1=table[r][:, GROUPS[g][0], :],
                op0=ALU.add,
                op1=ALU.mult,
            )

        def turn_back(g, a):
            tokens = slice(a * P, (a + 1) * P)
            bank = psum.tile([P, 4, P], F32, name="out_bank")
            for r in range(2):
                nc.tensor.transpose(bank[:, r, :], q1[g, r][:, tokens], ident[:])
            for r, other in ((2, 3), (3, 2)):
                for addend, first in ((SUM, True), (other, False)):
                    nc.tensor.matmul(
                        bank[:, r, :],
                        lhsT=products[g, addend][:, tokens],
                        rhs=ident[:],
                        start=first,
                        stop=not first,
                        is_transpose=True,
                    )
            out_banks[g, a] = bank

        def store(g, a):
            last = g == len(GROUPS) - 1
            if g not in result:
                result[g] = work.tile([P, TILES, E], F32, name="result", bufs=3)
                tiles_done[g] = 0
            source = out_banks[g, a][:].rearrange("p r (h i) -> p h r i", h=H)
            target = result[g][:, a, :].rearrange("p (h r i) -> p h r i", h=H, r=4)
            if (a == TILES - 1 and g % 4 < 2) or (last and a % 2 == 1):
                nc.vector.tensor_copy(out=target, in_=source)
            else:
                nc.scalar.copy(out=target, in_=source)
            tiles_done[g] += 1
            quarter, b = GROUPS[g]
            if last:
                nc.sync.dma_start(out=out_view[b, quarter][:, E * a : E * (a + 1)], in_=result[g][:, a, :])
            elif tiles_done[g] == TILES:
                nc.sync.dma_start(out=out_view[b, quarter], in_=result[g][:].rearrange("p a f -> p (a f)"))

        stages = {
            "scale_x": scale_x,
            "turn_x": turn_x,
            "empty_x": empty_x,
            "quantise_x": quantise_x,
            "down": down,
            "latent": latent,
            "interleave": interleave,
            "quantise_q": quantise_q,
            "up": up,
            "bias_q1": bias_q1,
            "rotate": rotate,
            "turn_back": turn_back,
            "store": store,
        }

        one_time = {
            -2: [lambda: turn_weights(w_down[:], "down")],
            0: [sines, lambda: quantise_weights("down")],
            1: [tables, lambda: [load_x(g) for g in range(EARLY_LOADS, len(GROUPS))]],
            2: [prepare_up],
        }
        angles()
        for step in range(min(min(LAGS), *one_time), len(GROUPS) + max(LAGS)):
            for job in one_time.get(step, []):
                job()
            for name, lag, *args in ORDER:
                g = step - lag
                if 0 <= g < len(GROUPS):
                    stages[name](g, *args)
